import numpy as np
import ml_dtypes


def mxq(x, axis, fmt="e4m3"):
    dtype, down = {"e4m3": (ml_dtypes.float8_e4m3fn, 7), "e5m2": (ml_dtypes.float8_e5m2, 14)}[fmt]
    v = np.moveaxis(np.asarray(x, np.float32).astype(ml_dtypes.bfloat16).astype(np.float64), axis, -1)
    blocks = v.reshape(v.shape[:-1] + (-1, 32))
    amax = np.abs(blocks).max(-1, keepdims=True)
    byte = np.maximum(np.where(amax > 0, np.frexp(amax)[1] - 1 + 127, 0) - down, 1)
    scale = np.exp2(byte - 127.0)
    codes = (blocks / scale).astype(np.float32).astype(dtype).astype(np.float64)
    return np.moveaxis((codes * scale).reshape(v.shape), -1, axis)


WIDE = False


def mx_kscale(k):
    if not WIDE:
        return np.ones(k)
    levels = np.array([10, -10, 5, -5, 0])
    a = np.random.permutation(np.resize(levels, k // 512 * 4)).reshape(k // 512, 4)
    idx = np.arange(k)
    return np.exp2(a[idx // 512, idx % 128 // 32])


BF16 = ml_dtypes.bfloat16


def bf(x):
    return np.asarray(x, np.float32).astype(BF16)


def f64(x):
    return np.asarray(x).astype(np.float64)


N, C, O, OH, OW, KH, KW, STRIDE, PAD = 32, 512, 128, 2, 2, 3, 3, 1, 1
H, W = (OH - 1) * STRIDE + KH - 2 * PAD, (OW - 1) * STRIDE + KW - 2 * PAD
NEG_SLOPE = 0.1


def span(t, n_out, n_in):
    ok = [p for p in range(n_out) if 0 <= p * STRIDE + t - PAD < n_in]
    return ok[0], ok[-1] + 1


def setup_inputs():
    s = mx_kscale(C)
    return {"x": bf(np.random.standard_normal((N, C, H, W)) * s[None, :, None, None]),
            "weight": bf(np.random.standard_normal((1, O, C, OH, OW, KH * KW)) * np.sqrt(2.0 / (KH * KW * C)) / s[None, None, :, None, None, None]),
            "bias": bf(np.random.standard_normal((1, O, OH, OW)) * 0.3)}


def reference(x, weight, bias):
    xq = mxq(f64(x), 1, "e4m3")
    wt = f64(weight)[0]
    acc = np.zeros((N, O, OH, OW))
    for i in range(KH):
        h0, h1 = span(i, OH, H)
        a0 = h0 * STRIDE + i - PAD
        for j in range(KW):
            w0, w1 = span(j, OW, W)
            b0 = w0 * STRIDE + j - PAD
            xs = xq[:, :, a0:a0 + (h1 - h0 - 1) * STRIDE + 1:STRIDE, b0:b0 + (w1 - w0 - 1) * STRIDE + 1:STRIDE]
            wq = mxq(wt[:, :, h0:h1, w0:w1, i * KW + j], 1, "e4m3")
            p = xs.transpose(2, 3, 0, 1) @ wq.transpose(2, 3, 1, 0)
            acc[:, :, h0:h1, w0:w1] += p.transpose(2, 3, 0, 1)
    out = acc + f64(bias)
    return np.where(out >= 0, out, NEG_SLOPE * out)

@@ -1,0 +1,151 @@
+from contextlib import ExitStack
+
+import concourse.mybir as mybir
+from concourse.masks import make_identity
+
+BF16 = mybir.dt.bfloat16
+F32 = mybir.dt.float32
+U32 = mybir.dt.uint32
+U8 = mybir.dt.uint8
+FP8X4 = mybir.dt.float8_e4m3fn_x4
+ALU = mybir.AluOpType
+
+P = 128
+PACK = 4
+BATCH = 32
+OUT_CH = 128
+PLACES = 4
+ENTRIES = 36
+GROUPS = 4
+RUN = 32
+NEG_SLOPE = 0.1
+
+O_HALF = 64
+HALVES = OUT_CH // O_HALF
+COLS = PLACES * O_HALF
+GROUPS_PER_LOAD = 2
+LOAD_RUN = GROUPS_PER_LOAD * RUN * ENTRIES
+
+FLOPS = 2 * BATCH * OUT_CH * PLACES * PLACES * 512
+BYTES = 2 * (OUT_CH * 512 * PLACES * PLACES + BATCH * 512 * PLACES + OUT_CH * PLACES) + 4 * BATCH * OUT_CH * PLACES
+
+
+def first_entry(h, w):
+    return 15 * h + 8 * w + 4
+
+
+def tile_locallyconnected2d_s_kernel(tc, x, weight, bias, out):
+    nc = tc.nc
+    with ExitStack() as ctx:
+        keep = ctx.enter_context(tc.tile_pool(name="keep", bufs=1))
+        loaded = ctx.enter_context(tc.tile_pool(name="loaded", bufs=HALVES * GROUPS // GROUPS_PER_LOAD))
+        work = ctx.enter_context(tc.tile_pool(name="work", bufs=3))
+        x_bank = ctx.enter_context(tc.psum_pool(name="x_bank", bufs=1))
+        flip_banks = ctx.enter_context(tc.psum_pool(name="flip_banks", bufs=4))
+        sum_banks = ctx.enter_context(tc.psum_pool(name="sum_banks", bufs=HALVES))
+
+        x_rows = keep.tile([P, P * PLACES], BF16)
+        nc.sync.dma_start(out=x_rows[:], in_=x.rearrange("n (t c) a b -> (n t) (c a b)", t=PACK))
+
+        w_rows = weight.rearrange(
+            "one (j ol) (u e c) h w k -> (one j) (ol u) e (c h w k)", j=HALVES, u=2, e=2
+        )
+        pieces = []
+        for j in range(HALVES):
+            for first_group in range(0, GROUPS, GROUPS_PER_LOAD):
+                piece = loaded.tile([P, 2 * LOAD_RUN], BF16)
+                start = first_group * RUN * ENTRIES
+                nc.sync.dma_start(
+                    out=piece[:].rearrange("q (e c) -> q e c", e=2),
+                    in_=w_rows[j][:, :, start : start + LOAD_RUN],
+                )
+                pieces.append(piece)
+
+        bias_rows = keep.tile([BATCH, OUT_CH * PLACES], BF16)
+        nc.scalar.dma_start(
+            out=bias_rows[:], in_=bias.rearrange("one o h w -> (one o h w)").partition_broadcast(BATCH)
+        )
+
+        ident_bf16 = keep.tile([P, P], BF16)
+        make_identity(nc, ident_bf16[:])
+        ident_f32 = keep.tile([P, P], F32)
+        make_identity(nc, ident_f32[:])
+
+        x_sorted = keep.tile([P, P * PLACES], BF16)
+        nc.vector.tensor_copy(
+            out=x_sorted[:].rearrange("q (g s r) -> q g s r", g=GROUPS, s=PLACES),
+            in_=x_rows[:].rearrange("q (g r s) -> q g s r", g=GROUPS, s=PLACES),
+        )
+        x_grouped = keep.tile([P, GROUPS * P * PACK], BF16, align_bytes=64)
+        nc.vector.memset(x_grouped[:], 0.0)
+        x_flipped = x_bank.tile([P, GROUPS * P], BF16)
+        for g in range(GROUPS):
+            nc.tensor.transpose(x_flipped[:, g * P : (g + 1) * P], x_sorted[:, g * P : (g + 1) * P], ident_bf16[:])
+        nc.vector.tensor_copy(
+            out=x_grouped[:].rearrange("p (g c) -> p g c", g=GROUPS)[:, :, 0 : BATCH * PACK],
+            in_=x_flipped[:].rearrange("p (g c) -> p g c", g=GROUPS),
+        )
+        x_codes = keep.tile([P, GROUPS * P], U32, align_bytes=64)
+        x_scales = keep.tile([P, GROUPS * P], U8, align_bytes=64)
+        nc.vector.quantize_mx(out=x_codes[:].bitcast(FP8X4), scales=x_scales[:], in_=x_grouped[:])
+
+        out_rows = out.rearrange("n o h w -> n (o h w)")
+        for j in range(HALVES):
+            sums = sum_banks.tile([P, COLS], F32)
+            for g in range(GROUPS):
+                piece = pieces[(j * GROUPS + g) // GROUPS_PER_LOAD]
+                entries = piece[:].rearrange(
+                    "q (e g r i) -> q e g r i", e=2, g=GROUPS_PER_LOAD, r=RUN
+                )[:, :, g % GROUPS_PER_LOAD, :, :]
+
+                w_sorted = work.tile([P, PLACES * P * 2], BF16)
+                for h in range(2):
+                    for w in range(2):
+                        hw = 2 * h + w
+                        taps = entries[:, :, :, first_entry(h, w) : first_entry(h, w) + 6].rearrange(
+                            "q e r (a k) -> q e r a k", a=2
+                        )[:, :, :, :, 0:2]
+                        nc.vector.tensor_copy(
+                            out=w_sorted[:, hw * 2 * P : (hw + 1) * 2 * P].rearrange(
+                                "q (a b r e) -> q a b r e", a=2, b=2, r=RUN
+                            ),
+                            in_=taps.rearrange("q e r a b -> q a b r e"),
+                        )
+
+                w_flipped = flip_banks.tile([P, PLACES * P], F32)
+                for hw in range(PLACES):
+                    nc.tensor.transpose(
+                        w_flipped[:, hw * P : (hw + 1) * P],
+                        w_sorted[:].bitcast(F32)[:, hw * P : (hw + 1) * P],
+                        ident_f32[:],
+                    )
+                w_grouped = work.tile([P, COLS * PACK], BF16, align_bytes=64)
+                nc.scalar.copy(out=w_grouped[:].bitcast(F32), in_=w_flipped[:])
+
+                w_codes = work.tile([P, COLS], U32, align_bytes=64)
+                w_scales = work.tile([P, COLS], U8, align_bytes=64)
+                nc.vector.quantize_mx(out=w_codes[:].bitcast(FP8X4), scales=w_scales[:], in_=w_grouped[:])
+
+                nc.tensor.matmul_mx(
+                    out=sums[:],
+                    lhsT=x_codes[:, g * P : (g + 1) * P].bitcast(FP8X4),
+                    lhsT_scale=x_scales[:, g * P : (g + 1) * P],
+                    rhs=w_codes[:].bitcast(FP8X4),
+                    rhs_scale=w_scales[:],
+                    start=(g == 0),
+                    stop=(g == GROUPS - 1),
+                )
+
+            o_cols = slice(j * COLS, (j + 1) * COLS)
+            biased = work.tile([BATCH, COLS], F32)
+            nc.vector.tensor_tensor(
+                out=biased[:].rearrange("n (ol hw) -> n ol hw", hw=PLACES),
+                in0=sums[0:BATCH, :].rearrange("n (hw ol) -> n ol hw", hw=PLACES),
+                in1=bias_rows[:, o_cols].rearrange("n (ol hw) -> n ol hw", hw=PLACES),
+                op=ALU.add,
+            )
+            result = work.tile([BATCH, COLS], F32)
+            nc.vector.scalar_tensor_tensor(
+                out=result[:], in0=biased[:], scalar=NEG_SLOPE, in1=biased[:], op0=ALU.mult, op1=ALU.max
+            )
+            nc.sync.dma_start(out=out_rows[:, o_cols], in_=result[:])

@@ -16,126 +16,97 @@ BATCH = 32
 OUT_CH = 128
 PLACES = 4
 ENTRIES = 36
-GROUPS = 4
-RUN = 32
 NEG_SLOPE = 0.1
 
-O_HALF = 64
-HALVES = OUT_CH // O_HALF
-COLS = PLACES * O_HALF
-GROUPS_PER_LOAD = 2
-LOAD_RUN = GROUPS_PER_LOAD * RUN * ENTRIES
+O_CHUNK = P // PACK
+CHUNKS = OUT_CH // O_CHUNK
+COLS = PLACES * O_CHUNK
 
 FLOPS = 2 * BATCH * OUT_CH * PLACES * PLACES * 512
 BYTES = 2 * (OUT_CH * 512 * PLACES * PLACES + BATCH * 512 * PLACES + OUT_CH * PLACES) + 4 * BATCH * OUT_CH * PLACES
 
 
-def first_entry(h, w):
-    return 15 * h + 8 * w + 4
+def entry(hw, s):
+    h, w = divmod(hw, 2)
+    a, b = divmod(s, 2)
+    return 15 * h + 8 * w + 3 * a + b + 4
 
 
 def tile_locallyconnected2d_s_kernel(tc, x, weight, bias, out):
     nc = tc.nc
     with ExitStack() as ctx:
         keep = ctx.enter_context(tc.tile_pool(name="keep", bufs=1))
-        loaded = ctx.enter_context(tc.tile_pool(name="loaded", bufs=HALVES * GROUPS // GROUPS_PER_LOAD))
-        work = ctx.enter_context(tc.tile_pool(name="work", bufs=3))
+        loaded = ctx.enter_context(tc.tile_pool(name="loaded", bufs=CHUNKS))
+        quantised = ctx.enter_context(tc.tile_pool(name="quantised", bufs=2))
+        work = ctx.enter_context(tc.tile_pool(name="work", bufs=4))
         x_bank = ctx.enter_context(tc.psum_pool(name="x_bank", bufs=1))
         flip_banks = ctx.enter_context(tc.psum_pool(name="flip_banks", bufs=4))
-        sum_banks = ctx.enter_context(tc.psum_pool(name="sum_banks", bufs=HALVES))
+        sum_banks = ctx.enter_context(tc.psum_pool(name="sum_banks", bufs=2))
+        ctx.enter_context(tc.manual_schedule())
 
         x_rows = keep.tile([P, P * PLACES], BF16)
         nc.sync.dma_start(out=x_rows[:], in_=x.rearrange("n (t c) a b -> (n t) (c a b)", t=PACK))
-
-        w_rows = weight.rearrange(
-            "one (j ol) (u e c) h w k -> (one j) (ol u) e (c h w k)", j=HALVES, u=2, e=2
-        )
+        w_rows = weight.rearrange("one (j ol) (t c) h w k -> (one j) (ol t) (c h w k)", j=CHUNKS, t=PACK)
         pieces = []
-        for j in range(HALVES):
-            for first_group in range(0, GROUPS, GROUPS_PER_LOAD):
-                piece = loaded.tile([P, 2 * LOAD_RUN], BF16)
-                start = first_group * RUN * ENTRIES
-                nc.sync.dma_start(
-                    out=piece[:].rearrange("q (e c) -> q e c", e=2),
-                    in_=w_rows[j][:, :, start : start + LOAD_RUN],
-                )
-                pieces.append(piece)
-
+        for j in range(CHUNKS):
+            piece = loaded.tile([P, P * ENTRIES], BF16)
+            nc.sync.dma_start(out=piece[:], in_=w_rows[j])
+            pieces.append(piece)
         bias_rows = keep.tile([BATCH, OUT_CH * PLACES], BF16)
         nc.scalar.dma_start(
             out=bias_rows[:], in_=bias.rearrange("one o h w -> (one o h w)").partition_broadcast(BATCH)
         )
+        ident = keep.tile([P, P], BF16)
+        make_identity(nc, ident[:])
 
-        ident_bf16 = keep.tile([P, P], BF16)
-        make_identity(nc, ident_bf16[:])
-        ident_f32 = keep.tile([P, P], F32)
-        make_identity(nc, ident_f32[:])
-
-        x_sorted = keep.tile([P, P * PLACES], BF16)
-        nc.vector.tensor_copy(
-            out=x_sorted[:].rearrange("q (g s r) -> q g s r", g=GROUPS, s=PLACES),
-            in_=x_rows[:].rearrange("q (g r s) -> q g s r", g=GROUPS, s=PLACES),
-        )
-        x_grouped = keep.tile([P, GROUPS * P * PACK], BF16, align_bytes=64)
+        x_grouped = keep.tile([P, PLACES * P * PACK], BF16, align_bytes=64)
         nc.vector.memset(x_grouped[:], 0.0)
-        x_flipped = x_bank.tile([P, GROUPS * P], BF16)
-        for g in range(GROUPS):
-            nc.tensor.transpose(x_flipped[:, g * P : (g + 1) * P], x_sorted[:, g * P : (g + 1) * P], ident_bf16[:])
+        x_flipped = x_bank.tile([P, PLACES * P], BF16)
+        for s in range(PLACES):
+            nc.tensor.transpose(
+                x_flipped[:, s * P : (s + 1) * P],
+                x_rows[:].rearrange("q (c s) -> q c s", s=PLACES)[:, :, s],
+                ident[:],
+            )
         nc.vector.tensor_copy(
-            out=x_grouped[:].rearrange("p (g c) -> p g c", g=GROUPS)[:, :, 0 : BATCH * PACK],
-            in_=x_flipped[:].rearrange("p (g c) -> p g c", g=GROUPS),
+            out=x_grouped[:].rearrange("p (s c) -> p s c", s=PLACES)[:, :, 0 : BATCH * PACK],
+            in_=x_flipped[:].rearrange("p (s c) -> p s c", s=PLACES),
         )
-        x_codes = keep.tile([P, GROUPS * P], U32, align_bytes=64)
-        x_scales = keep.tile([P, GROUPS * P], U8, align_bytes=64)
+        x_codes = keep.tile([P, PLACES * P], U32, align_bytes=64)
+        x_scales = keep.tile([P, PLACES * P], U8, align_bytes=64)
         nc.vector.quantize_mx(out=x_codes[:].bitcast(FP8X4), scales=x_scales[:], in_=x_grouped[:])
 
         out_rows = out.rearrange("n o h w -> n (o h w)")
-        for j in range(HALVES):
-            sums = sum_banks.tile([P, COLS], F32)
-            for g in range(GROUPS):
-                piece = pieces[(j * GROUPS + g) // GROUPS_PER_LOAD]
-                entries = piece[:].rearrange(
-                    "q (e g r i) -> q e g r i", e=2, g=GROUPS_PER_LOAD, r=RUN
-                )[:, :, g % GROUPS_PER_LOAD, :, :]
 
-                w_sorted = work.tile([P, PLACES * P * 2], BF16)
-                for h in range(2):
-                    for w in range(2):
-                        hw = 2 * h + w
-                        taps = entries[:, :, :, first_entry(h, w) : first_entry(h, w) + 6].rearrange(
-                            "q e r (a k) -> q e r a k", a=2
-                        )[:, :, :, :, 0:2]
-                        nc.vector.tensor_copy(
-                            out=w_sorted[:, hw * 2 * P : (hw + 1) * 2 * P].rearrange(
-                                "q (a b r e) -> q a b r e", a=2, b=2, r=RUN
-                            ),
-                            in_=taps.rearrange("q e r a b -> q a b r e"),
-                        )
-
-                w_flipped = flip_banks.tile([P, PLACES * P], F32)
+        def flip_and_quantise(j):
+            entries = pieces[j][:].rearrange("q (c i) -> q c i", i=ENTRIES)
+            w_codes = quantised.tile([P, PLACES * COLS], U32, align_bytes=64)
+            w_scales = quantised.tile([P, PLACES * COLS], U8, align_bytes=64)
+            for s in range(PLACES):
+                w_flipped = flip_banks.tile([P, COLS * PACK], BF16)
                 for hw in range(PLACES):
-                    nc.tensor.transpose(
-                        w_flipped[:, hw * P : (hw + 1) * P],
-                        w_sorted[:].bitcast(F32)[:, hw * P : (hw + 1) * P],
-                        ident_f32[:],
-                    )
+                    nc.tensor.transpose(w_flipped[:, hw * P : (hw + 1) * P], entries[:, :, entry(hw, s)], ident[:])
                 w_grouped = work.tile([P, COLS * PACK], BF16, align_bytes=64)
-                nc.scalar.copy(out=w_grouped[:].bitcast(F32), in_=w_flipped[:])
+                nc.scalar.copy(out=w_grouped[:], in_=w_flipped[:])
+                nc.vector.quantize_mx(
+                    out=w_codes[:, s * COLS : (s + 1) * COLS].bitcast(FP8X4),
+                    scales=w_scales[:, s * COLS : (s + 1) * COLS],
+                    in_=w_grouped[:],
+                )
+            return w_codes, w_scales
 
-                w_codes = work.tile([P, COLS], U32, align_bytes=64)
-                w_scales = work.tile([P, COLS], U8, align_bytes=64)
-                nc.vector.quantize_mx(out=w_codes[:].bitcast(FP8X4), scales=w_scales[:], in_=w_grouped[:])
-
+        def multiply_and_store(j, w_codes, w_scales):
+            sums = sum_banks.tile([P, COLS], F32)
+            for s in range(PLACES):
                 nc.tensor.matmul_mx(
                     out=sums[:],
-                    lhsT=x_codes[:, g * P : (g + 1) * P].bitcast(FP8X4),
-                    lhsT_scale=x_scales[:, g * P : (g + 1) * P],
-                    rhs=w_codes[:].bitcast(FP8X4),
-                    rhs_scale=w_scales[:],
-                    start=(g == 0),
-                    stop=(g == GROUPS - 1),
+                    lhsT=x_codes[:, s * P : (s + 1) * P].bitcast(FP8X4),
+                    lhsT_scale=x_scales[:, s * P : (s + 1) * P],
+                    rhs=w_codes[:, s * COLS : (s + 1) * COLS].bitcast(FP8X4),
+                    rhs_scale=w_scales[:, s * COLS : (s + 1) * COLS],
+                    start=(s == 0),
+                    stop=(s == PLACES - 1),
                 )
-
             o_cols = slice(j * COLS, (j + 1) * COLS)
             biased = work.tile([BATCH, COLS], F32)
             nc.vector.tensor_tensor(
@@ -149,3 +120,10 @@ def tile_locallyconnected2d_s_kernel(tc, x, weight, bias, out):
                 out=result[:], in0=biased[:], scalar=NEG_SLOPE, in1=biased[:], op0=ALU.mult, op1=ALU.max
             )
             nc.sync.dma_start(out=out_rows[:, o_cols], in_=result[:])
+
+        ready = flip_and_quantise(0)
+        for j in range(1, CHUNKS):
+            following = flip_and_quantise(j)
+            multiply_and_store(j - 1, ready[0], ready[1])
+            ready = following
+        multiply_and_store(CHUNKS - 1, ready[0], ready[1])

@@ -21,6 +21,7 @@ NEG_SLOPE = 0.1
 O_CHUNK = P // PACK
 CHUNKS = OUT_CH // O_CHUNK
 COLS = PLACES * O_CHUNK
+IDLE_PASSES = 2
 
 FLOPS = 2 * BATCH * OUT_CH * PLACES * PLACES * 512
 BYTES = 2 * (OUT_CH * 512 * PLACES * PLACES + BATCH * 512 * PLACES + OUT_CH * PLACES) + 4 * BATCH * OUT_CH * PLACES
@@ -42,6 +43,7 @@ def tile_locallyconnected2d_s_kernel(tc, x, weight, bias, out):
         x_bank = ctx.enter_context(tc.psum_pool(name="x_bank", bufs=1))
         flip_banks = ctx.enter_context(tc.psum_pool(name="flip_banks", bufs=4))
         sum_banks = ctx.enter_context(tc.psum_pool(name="sum_banks", bufs=2))
+        idle_bank = ctx.enter_context(tc.psum_pool(name="idle_bank", bufs=1))
         ctx.enter_context(tc.manual_schedule())
 
         x_rows = keep.tile([P, P * PLACES], BF16)
@@ -77,6 +79,20 @@ def tile_locallyconnected2d_s_kernel(tc, x, weight, bias, out):
         nc.vector.quantize_mx(out=x_codes[:].bitcast(FP8X4), scales=x_scales[:], in_=x_grouped[:])
 
         out_rows = out.rearrange("n o h w -> n (o h w)")
+
+        unread = idle_bank.tile([P, PLACES * P], F32)
+
+        def keep_clock_up():
+            for i in range(IDLE_PASSES):
+                nc.tensor.matmul_mx(
+                    out=unread[:],
+                    lhsT=x_codes[:, 0:P].bitcast(FP8X4),
+                    lhsT_scale=x_scales[:, 0:P],
+                    rhs=x_codes[:].bitcast(FP8X4),
+                    rhs_scale=x_scales[:],
+                    start=True,
+                    stop=True,
+                )
 
         def flip_and_quantise(j):
             entries = pieces[j][:].rearrange("q (c i) -> q c i", i=ENTRIES)
@@ -121,8 +137,10 @@ def tile_locallyconnected2d_s_kernel(tc, x, weight, bias, out):
             )
             nc.sync.dma_start(out=out_rows[:, o_cols], in_=result[:])
 
+        keep_clock_up()
         ready = flip_and_quantise(0)
         for j in range(1, CHUNKS):
+            keep_clock_up()
             following = flip_and_quantise(j)
             multiply_and_store(j - 1, ready[0], ready[1])
             ready = following

@@ -21,15 +21,12 @@ NEG_SLOPE = 0.1
 O_CHUNK = P // PACK
 CHUNKS = OUT_CH // O_CHUNK
 COLS = PLACES * O_CHUNK
-IDLE_PASSES = 2
 
 FLOPS = 2 * BATCH * OUT_CH * PLACES * PLACES * 512
 BYTES = 2 * (OUT_CH * 512 * PLACES * PLACES + BATCH * 512 * PLACES + OUT_CH * PLACES) + 4 * BATCH * OUT_CH * PLACES
 
 
-def entry(hw, s):
-    h, w = divmod(hw, 2)
-    a, b = divmod(s, 2)
+def entry(h, w, a, b):
     return 15 * h + 8 * w + 3 * a + b + 4
 
 
@@ -39,11 +36,11 @@ def tile_locallyconnected2d_s_kernel(tc, x, weight, bias, out):
         keep = ctx.enter_context(tc.tile_pool(name="keep", bufs=1))
         loaded = ctx.enter_context(tc.tile_pool(name="loaded", bufs=CHUNKS))
         quantised = ctx.enter_context(tc.tile_pool(name="quantised", bufs=2))
-        work = ctx.enter_context(tc.tile_pool(name="work", bufs=4))
+        work = ctx.enter_context(tc.tile_pool(name="work", bufs=3))
         x_bank = ctx.enter_context(tc.psum_pool(name="x_bank", bufs=1))
-        flip_banks = ctx.enter_context(tc.psum_pool(name="flip_banks", bufs=4))
+        whole_banks = ctx.enter_context(tc.psum_pool(name="whole_banks", bufs=2))
+        split_banks = ctx.enter_context(tc.psum_pool(name="split_banks", bufs=2))
         sum_banks = ctx.enter_context(tc.psum_pool(name="sum_banks", bufs=2))
-        idle_bank = ctx.enter_context(tc.psum_pool(name="idle_bank", bufs=1))
         ctx.enter_context(tc.manual_schedule())
 
         x_rows = keep.tile([P, P * PLACES], BF16)
@@ -58,8 +55,10 @@ def tile_locallyconnected2d_s_kernel(tc, x, weight, bias, out):
         nc.scalar.dma_start(
             out=bias_rows[:], in_=bias.rearrange("one o h w -> (one o h w)").partition_broadcast(BATCH)
         )
-        ident = keep.tile([P, P], BF16)
-        make_identity(nc, ident[:])
+        ident_bf16 = keep.tile([P, P], BF16)
+        make_identity(nc, ident_bf16[:])
+        ident_f32 = keep.tile([P, P], F32)
+        make_identity(nc, ident_f32[:])
 
         x_grouped = keep.tile([P, PLACES * P * PACK], BF16, align_bytes=64)
         nc.vector.memset(x_grouped[:], 0.0)
@@ -68,7 +67,7 @@ def tile_locallyconnected2d_s_kernel(tc, x, weight, bias, out):
             nc.tensor.transpose(
                 x_flipped[:, s * P : (s + 1) * P],
                 x_rows[:].rearrange("q (c s) -> q c s", s=PLACES)[:, :, s],
-                ident[:],
+                ident_bf16[:],
             )
         nc.vector.tensor_copy(
             out=x_grouped[:].rearrange("p (s c) -> p s c", s=PLACES)[:, :, 0 : BATCH * PACK],
@@ -80,34 +79,43 @@ def tile_locallyconnected2d_s_kernel(tc, x, weight, bias, out):
 
         out_rows = out.rearrange("n o h w -> n (o h w)")
 
-        unread = idle_bank.tile([P, PLACES * P], F32)
-
-        def keep_clock_up():
-            for i in range(IDLE_PASSES):
-                nc.tensor.matmul_mx(
-                    out=unread[:],
-                    lhsT=x_codes[:, 0:P].bitcast(FP8X4),
-                    lhsT_scale=x_scales[:, 0:P],
-                    rhs=x_codes[:].bitcast(FP8X4),
-                    rhs_scale=x_scales[:],
-                    start=True,
-                    stop=True,
-                )
-
         def flip_and_quantise(j):
-            entries = pieces[j][:].rearrange("q (c i) -> q c i", i=ENTRIES)
+            words = pieces[j][:].bitcast(F32).rearrange("q (c k) -> q c k", k=ENTRIES // 2)
             w_codes = quantised.tile([P, PLACES * COLS], U32, align_bytes=64)
             w_scales = quantised.tile([P, PLACES * COLS], U8, align_bytes=64)
-            for s in range(PLACES):
-                w_flipped = flip_banks.tile([P, COLS * PACK], BF16)
-                for hw in range(PLACES):
-                    nc.tensor.transpose(w_flipped[:, hw * P : (hw + 1) * P], entries[:, :, entry(hw, s)], ident[:])
-                w_grouped = work.tile([P, COLS * PACK], BF16, align_bytes=64)
-                nc.scalar.copy(out=w_grouped[:], in_=w_flipped[:])
+            grouped_tiles = []
+            for a in range(2):
+                whole = whole_banks.tile([P, 2 * P], F32)
+                for w in range(2):
+                    nc.tensor.transpose(
+                        whole[:, w * P : (w + 1) * P], words[:, :, entry(a, w, a, 0) // 2], ident_f32[:]
+                    )
+                split = split_banks.tile([P, 4 * P], F32)
+                for w in range(2):
+                    for b in range(2):
+                        nc.tensor.transpose(
+                            split[:, (2 * w + b) * P : (2 * w + b + 1) * P],
+                            words[:, :, entry(1 - a, w, a, b) // 2],
+                            ident_f32[:],
+                        )
+
+                w_grouped = work.tile([P, 2 * COLS * PACK], BF16, align_bytes=64)
+                grouped = w_grouped[:].rearrange("p (b h w c) -> p b h w c", b=2, h=2, w=2)
+                whole_halves = whole[:].bitcast(BF16).rearrange("p (w c b) -> p b w c", w=2, b=2)
+                if a == 0:
+                    nc.scalar.copy(out=grouped[:, :, a, :, :], in_=whole_halves)
+                else:
+                    nc.vector.tensor_copy(out=grouped[:, :, a, :, :], in_=whole_halves)
+                split_halves = split[:].bitcast(BF16).rearrange("p (w b c e) -> p w b c e", w=2, b=2, e=2)
+                for b in range(2):
+                    nc.scalar.copy(out=grouped[:, b, 1 - a, :, :], in_=split_halves[:, :, b, :, 1 - b])
+                grouped_tiles.append(w_grouped)
+
+            for a in range(2):
                 nc.vector.quantize_mx(
-                    out=w_codes[:, s * COLS : (s + 1) * COLS].bitcast(FP8X4),
-                    scales=w_scales[:, s * COLS : (s + 1) * COLS],
-                    in_=w_grouped[:],
+                    out=w_codes[:, 2 * a * COLS : 2 * (a + 1) * COLS].bitcast(FP8X4),
+                    scales=w_scales[:, 2 * a * COLS : 2 * (a + 1) * COLS],
+                    in_=grouped_tiles[a][:],
                 )
             return w_codes, w_scales
 
@@ -137,10 +145,8 @@ def tile_locallyconnected2d_s_kernel(tc, x, weight, bias, out):
             )
             nc.sync.dma_start(out=out_rows[:, o_cols], in_=result[:])
 
-        keep_clock_up()
         ready = flip_and_quantise(0)
         for j in range(1, CHUNKS):
-            keep_clock_up()
             following = flip_and_quantise(j)
             multiply_and_store(j - 1, ready[0], ready[1])
             ready = following

@@ -35,7 +35,7 @@ def tile_locallyconnected2d_s_kernel(tc, x, weight, bias, out):
     with ExitStack() as ctx:
         keep = ctx.enter_context(tc.tile_pool(name="keep", bufs=1))
         loaded = ctx.enter_context(tc.tile_pool(name="loaded", bufs=CHUNKS))
-        quantised = ctx.enter_context(tc.tile_pool(name="quantised", bufs=2))
+        quantised = ctx.enter_context(tc.tile_pool(name="quantised", bufs=CHUNKS))
         work = ctx.enter_context(tc.tile_pool(name="work", bufs=3))
         x_bank = ctx.enter_context(tc.psum_pool(name="x_bank", bufs=1))
         whole_banks = ctx.enter_context(tc.psum_pool(name="whole_banks", bufs=2))
@@ -145,9 +145,9 @@ def tile_locallyconnected2d_s_kernel(tc, x, weight, bias, out):
             )
             nc.sync.dma_start(out=out_rows[:, o_cols], in_=result[:])
 
-        ready = flip_and_quantise(0)
-        for j in range(1, CHUNKS):
-            following = flip_and_quantise(j)
-            multiply_and_store(j - 1, ready[0], ready[1])
-            ready = following
-        multiply_and_store(CHUNKS - 1, ready[0], ready[1])
+        ready = [flip_and_quantise(j) for j in range(3)]
+        for j in range(2):
+            multiply_and_store(j, ready[j][0], ready[j][1])
+        ready.append(flip_and_quantise(3))
+        for j in range(2, CHUNKS):
+            multiply_and_store(j, ready[j][0], ready[j][1])

@@ -119,35 +119,37 @@ def tile_locallyconnected2d_s_kernel(tc, x, weight, bias, out):
                 )
             return w_codes, w_scales
 
-        def multiply_and_store(j, w_codes, w_scales):
-            sums = sum_banks.tile([P, COLS], F32)
-            for s in range(PLACES):
-                nc.tensor.matmul_mx(
-                    out=sums[:],
-                    lhsT=x_codes[:, s * P : (s + 1) * P].bitcast(FP8X4),
-                    lhsT_scale=x_scales[:, s * P : (s + 1) * P],
-                    rhs=w_codes[:, s * COLS : (s + 1) * COLS].bitcast(FP8X4),
-                    rhs_scale=w_scales[:, s * COLS : (s + 1) * COLS],
-                    start=(s == 0),
-                    stop=(s == PLACES - 1),
-                )
-            o_cols = slice(j * COLS, (j + 1) * COLS)
-            biased = work.tile([BATCH, COLS], F32)
+        def multiply_and_store(first, operands):
+            count = len(operands)
+            sums = sum_banks.tile([P, count * COLS], F32)
+            for i in range(count):
+                w_codes, w_scales = operands[i]
+                for s in range(PLACES):
+                    nc.tensor.matmul_mx(
+                        out=sums[:, i * COLS : (i + 1) * COLS],
+                        lhsT=x_codes[:, s * P : (s + 1) * P].bitcast(FP8X4),
+                        lhsT_scale=x_scales[:, s * P : (s + 1) * P],
+                        rhs=w_codes[:, s * COLS : (s + 1) * COLS].bitcast(FP8X4),
+                        rhs_scale=w_scales[:, s * COLS : (s + 1) * COLS],
+                        start=(s == 0),
+                        stop=(s == PLACES - 1),
+                    )
+            o_cols = slice(first * COLS, (first + count) * COLS)
+            biased = work.tile([BATCH, count * COLS], F32)
             nc.vector.tensor_tensor(
-                out=biased[:].rearrange("n (ol hw) -> n ol hw", hw=PLACES),
-                in0=sums[0:BATCH, :].rearrange("n (hw ol) -> n ol hw", hw=PLACES),
-                in1=bias_rows[:, o_cols].rearrange("n (ol hw) -> n ol hw", hw=PLACES),
+                out=biased[:].rearrange("n (j ol hw) -> n j ol hw", j=count, hw=PLACES),
+                in0=sums[0:BATCH, :].rearrange("n (j hw ol) -> n j ol hw", j=count, hw=PLACES),
+                in1=bias_rows[:, o_cols].rearrange("n (j ol hw) -> n j ol hw", j=count, hw=PLACES),
                 op=ALU.add,
             )
-            result = work.tile([BATCH, COLS], F32)
+            result = work.tile([BATCH, count * COLS], F32)
             nc.vector.scalar_tensor_tensor(
                 out=result[:], in0=biased[:], scalar=NEG_SLOPE, in1=biased[:], op0=ALU.mult, op1=ALU.max
             )
             nc.sync.dma_start(out=out_rows[:, o_cols], in_=result[:])
 
         ready = [flip_and_quantise(j) for j in range(3)]
-        for j in range(2):
-            multiply_and_store(j, ready[j][0], ready[j][1])
+        multiply_and_store(0, ready[0:2])
         ready.append(flip_and_quantise(3))
-        for j in range(2, CHUNKS):
-            multiply_and_store(j, ready[j][0], ready[j][1])
+        multiply_and_store(2, ready[2:3])
+        multiply_and_store(3, ready[3:4])

@@ -39,7 +39,7 @@ def tile_locallyconnected2d_s_kernel(tc, x, weight, bias, out):
         work = ctx.enter_context(tc.tile_pool(name="work", bufs=3))
         x_bank = ctx.enter_context(tc.psum_pool(name="x_bank", bufs=1))
         whole_banks = ctx.enter_context(tc.psum_pool(name="whole_banks", bufs=2))
-        split_banks = ctx.enter_context(tc.psum_pool(name="split_banks", bufs=2))
+        split_banks = ctx.enter_context(tc.psum_pool(name="split_banks", bufs=3))
         sum_banks = ctx.enter_context(tc.psum_pool(name="sum_banks", bufs=2))
         ctx.enter_context(tc.manual_schedule())
 
@@ -79,38 +79,70 @@ def tile_locallyconnected2d_s_kernel(tc, x, weight, bias, out):
 
         out_rows = out.rearrange("n o h w -> n (o h w)")
 
-        def flip_and_quantise(j):
+        def flip_and_quantise(j, shared):
             words = pieces[j][:].bitcast(F32).rearrange("q (c k) -> q c k", k=ENTRIES // 2)
             w_codes = quantised.tile([P, PLACES * COLS], U32, align_bytes=64)
             w_scales = quantised.tile([P, PLACES * COLS], U8, align_bytes=64)
             grouped_tiles = []
             for a in range(2):
+                w_grouped = work.tile([P, 2 * COLS * PACK], BF16, align_bytes=64)
+                grouped_tiles.append(w_grouped)
+
+            def grouped(a):
+                return grouped_tiles[a][:].rearrange("p (b h w c) -> p b h w c", b=2, h=2, w=2)
+
+            def flip_whole(a):
                 whole = whole_banks.tile([P, 2 * P], F32)
                 for w in range(2):
                     nc.tensor.transpose(
                         whole[:, w * P : (w + 1) * P], words[:, :, entry(a, w, a, 0) // 2], ident_f32[:]
                     )
-                split = split_banks.tile([P, 4 * P], F32)
-                for w in range(2):
-                    for b in range(2):
+                return whole
+
+            def flip_split(a, some_b):
+                split = split_banks.tile([P, 2 * len(some_b) * P], F32)
+                for i in range(len(some_b)):
+                    for w in range(2):
                         nc.tensor.transpose(
-                            split[:, (2 * w + b) * P : (2 * w + b + 1) * P],
-                            words[:, :, entry(1 - a, w, a, b) // 2],
+                            split[:, (2 * i + w) * P : (2 * i + w + 1) * P],
+                            words[:, :, entry(1 - a, w, a, some_b[i]) // 2],
                             ident_f32[:],
                         )
+                return split
 
-                w_grouped = work.tile([P, 2 * COLS * PACK], BF16, align_bytes=64)
-                grouped = w_grouped[:].rearrange("p (b h w c) -> p b h w c", b=2, h=2, w=2)
-                whole_halves = whole[:].bitcast(BF16).rearrange("p (w c b) -> p b w c", w=2, b=2)
-                if a == 0:
-                    nc.scalar.copy(out=grouped[:, :, a, :, :], in_=whole_halves)
-                else:
-                    nc.vector.tensor_copy(out=grouped[:, :, a, :, :], in_=whole_halves)
-                split_halves = split[:].bitcast(BF16).rearrange("p (w b c e) -> p w b c e", w=2, b=2, e=2)
-                for b in range(2):
-                    nc.scalar.copy(out=grouped[:, b, 1 - a, :, :], in_=split_halves[:, :, b, :, 1 - b])
-                grouped_tiles.append(w_grouped)
+            def copy_whole(copy, a, whole):
+                copy(
+                    out=grouped(a)[:, :, a, :, :],
+                    in_=whole[:].bitcast(BF16).rearrange("p (w c b) -> p b w c", w=2, b=2),
+                )
 
+            def copy_split(copy, a, b, split, i):
+                halves = split[:, 2 * i * P : 2 * (i + 1) * P].bitcast(BF16).rearrange("p (w c e) -> p w c e", w=2, e=2)
+                copy(out=grouped(a)[:, b, 1 - a, :, :], in_=halves[:, :, :, 1 - b])
+
+            if shared:
+                whole_0 = flip_whole(0)
+                whole_1 = flip_whole(1)
+                split_0 = flip_split(0, [0, 1])
+                split_10 = flip_split(1, [0])
+                split_11 = flip_split(1, [1])
+                copy_whole(nc.scalar.copy, 0, whole_0)
+                copy_split(nc.scalar.copy, 0, 0, split_0, 0)
+                copy_split(nc.scalar.copy, 0, 1, split_0, 1)
+                copy_split(nc.scalar.copy, 1, 1, split_11, 0)
+                copy_whole(nc.vector.tensor_copy, 1, whole_1)
+                copy_split(nc.vector.tensor_copy, 1, 0, split_10, 0)
+            else:
+                whole_0 = flip_whole(0)
+                split_0 = flip_split(0, [0, 1])
+                whole_1 = flip_whole(1)
+                split_1 = flip_split(1, [0, 1])
+                copy_whole(nc.scalar.copy, 0, whole_0)
+                copy_split(nc.scalar.copy, 0, 0, split_0, 0)
+                copy_split(nc.scalar.copy, 0, 1, split_0, 1)
+                copy_split(nc.scalar.copy, 1, 0, split_1, 0)
+                copy_split(nc.scalar.copy, 1, 1, split_1, 1)
+                copy_whole(nc.vector.tensor_copy, 1, whole_1)
             for a in range(2):
                 nc.vector.quantize_mx(
                     out=w_codes[:, 2 * a * COLS : 2 * (a + 1) * COLS].bitcast(FP8X4),
@@ -148,8 +180,8 @@ def tile_locallyconnected2d_s_kernel(tc, x, weight, bias, out):
             )
             nc.sync.dma_start(out=out_rows[:, o_cols], in_=result[:])
 
-        ready = [flip_and_quantise(j) for j in range(3)]
+        ready = [flip_and_quantise(j, False) for j in range(3)]
         multiply_and_store(0, ready[0:2])
-        ready.append(flip_and_quantise(3))
+        ready.append(flip_and_quantise(3, True))
         multiply_and_store(2, ready[2:3])
         multiply_and_store(3, ready[3:4])

@@ -127,8 +127,10 @@ def tile_locallyconnected2d_s_kernel(tc, x, weight, bias, out):
                 split_10 = flip_split(1, [0])
                 split_11 = flip_split(1, [1])
                 copy_whole(nc.scalar.copy, 0, whole_0)
-                copy_split(nc.scalar.copy, 0, 0, split_0, 0)
-                copy_split(nc.scalar.copy, 0, 1, split_0, 1)
+                nc.scalar.copy(
+                    out=grouped(0)[:, :, 1, :, :].rearrange("p b w c -> p b (w c)"),
+                    in_=split_0[:].bitcast(BF16)[:, 1 : 8 * P - 1].rearrange("p (b r) -> p b r", b=2)[:, :, 0 : 4 * P - 1 : 2],
+                )
                 copy_split(nc.scalar.copy, 1, 1, split_11, 0)
                 copy_whole(nc.vector.tensor_copy, 1, whole_1)
                 copy_split(nc.vector.tensor_copy, 1, 0, split_10, 0)
@@ -180,7 +182,7 @@ def tile_locallyconnected2d_s_kernel(tc, x, weight, bias, out):
             )
             nc.sync.dma_start(out=out_rows[:, o_cols], in_=result[:])
 
-        ready = [flip_and_quantise(j, False) for j in range(3)]
+        ready = [flip_and_quantise(j, True) for j in range(3)]
         multiply_and_store(0, ready[0:2])
         ready.append(flip_and_quantise(3, True))
         multiply_and_store(2, ready[2:3])

from contextlib import ExitStack

import concourse.mybir as mybir
from concourse.masks import make_identity

BF16 = mybir.dt.bfloat16
F32 = mybir.dt.float32
U32 = mybir.dt.uint32
U8 = mybir.dt.uint8
FP8X4 = mybir.dt.float8_e4m3fn_x4
ALU = mybir.AluOpType

P = 128
PACK = 4
BATCH = 32
OUT_CH = 128
PLACES = 4
ENTRIES = 36
NEG_SLOPE = 0.1

O_CHUNK = P // PACK
CHUNKS = OUT_CH // O_CHUNK
COLS = PLACES * O_CHUNK

FLOPS = 2 * BATCH * OUT_CH * PLACES * PLACES * 512
BYTES = 2 * (OUT_CH * 512 * PLACES * PLACES + BATCH * 512 * PLACES + OUT_CH * PLACES) + 4 * BATCH * OUT_CH * PLACES


def entry(h, w, a, b):
    return 15 * h + 8 * w + 3 * a + b + 4


def tile_locallyconnected2d_s_kernel(tc, x, weight, bias, out):
    nc = tc.nc
    with ExitStack() as ctx:
        keep = ctx.enter_context(tc.tile_pool(name="keep", bufs=1))
        loaded = ctx.enter_context(tc.tile_pool(name="loaded", bufs=CHUNKS))
        quantised = ctx.enter_context(tc.tile_pool(name="quantised", bufs=CHUNKS))
        work = ctx.enter_context(tc.tile_pool(name="work", bufs=3))
        x_bank = ctx.enter_context(tc.psum_pool(name="x_bank", bufs=1))
        whole_banks = ctx.enter_context(tc.psum_pool(name="whole_banks", bufs=2))
        split_banks = ctx.enter_context(tc.psum_pool(name="split_banks", bufs=3))
        sum_banks = ctx.enter_context(tc.psum_pool(name="sum_banks", bufs=2))
        ctx.enter_context(tc.manual_schedule())

        x_rows = keep.tile([P, P * PLACES], BF16)
        nc.sync.dma_start(out=x_rows[:], in_=x.rearrange("n (t c) a b -> (n t) (c a b)", t=PACK))
        w_rows = weight.rearrange("one (j ol) (t c) h w k -> (one j) (ol t) (c h w k)", j=CHUNKS, t=PACK)
        pieces = []
        for j in range(CHUNKS):
            piece = loaded.tile([P, P * ENTRIES], BF16)
            nc.sync.dma_start(out=piece[:], in_=w_rows[j])
            pieces.append(piece)
        bias_rows = keep.tile([BATCH, OUT_CH * PLACES], BF16)
        nc.scalar.dma_start(
            out=bias_rows[:], in_=bias.rearrange("one o h w -> (one o h w)").partition_broadcast(BATCH)
        )
        ident_bf16 = keep.tile([P, P], BF16)
        make_identity(nc, ident_bf16[:])
        ident_f32 = keep.tile([P, P], F32)
        make_identity(nc, ident_f32[:])

        x_grouped = keep.tile([P, PLACES * P * PACK], BF16, align_bytes=64)
        nc.vector.memset(x_grouped[:], 0.0)
        x_flipped = x_bank.tile([P, PLACES * P], BF16)
        for s in range(PLACES):
            nc.tensor.transpose(
                x_flipped[:, s * P : (s + 1) * P],
                x_rows[:].rearrange("q (c s) -> q c s", s=PLACES)[:, :, s],
                ident_bf16[:],
            )
        nc.vector.tensor_copy(
            out=x_grouped[:].rearrange("p (s c) -> p s c", s=PLACES)[:, :, 0 : BATCH * PACK],
            in_=x_flipped[:].rearrange("p (s c) -> p s c", s=PLACES),
        )
        x_codes = keep.tile([P, PLACES * P], U32, align_bytes=64)
        x_scales = keep.tile([P, PLACES * P], U8, align_bytes=64)
        nc.vector.quantize_mx(out=x_codes[:].bitcast(FP8X4), scales=x_scales[:], in_=x_grouped[:])

        out_rows = out.rearrange("n o h w -> n (o h w)")

        def flip_and_quantise(j, shared):
            words = pieces[j][:].bitcast(F32).rearrange("q (c k) -> q c k", k=ENTRIES // 2)
            w_codes = quantised.tile([P, PLACES * COLS], U32, align_bytes=64)
            w_scales = quantised.tile([P, PLACES * COLS], U8, align_bytes=64)
            grouped_tiles = []
            for a in range(2):
                w_grouped = work.tile([P, 2 * COLS * PACK], BF16, align_bytes=64)
                grouped_tiles.append(w_grouped)

            def grouped(a):
                return grouped_tiles[a][:].rearrange("p (b h w c) -> p b h w c", b=2, h=2, w=2)

            def flip_whole(a):
                whole = whole_banks.tile([P, 2 * P], F32)
                for w in range(2):
                    nc.tensor.transpose(
                        whole[:, w * P : (w + 1) * P], words[:, :, entry(a, w, a, 0) // 2], ident_f32[:]
                    )
                return whole

            def flip_split(a, some_b):
                split = split_banks.tile([P, 2 * len(some_b) * P], F32)
                for i in range(len(some_b)):
                    for w in range(2):
                        nc.tensor.transpose(
                            split[:, (2 * i + w) * P : (2 * i + w + 1) * P],
                            words[:, :, entry(1 - a, w, a, some_b[i]) // 2],
                            ident_f32[:],
                        )
                return split

            def copy_whole(copy, a, whole):
                copy(
                    out=grouped(a)[:, :, a, :, :],
                    in_=whole[:].bitcast(BF16).rearrange("p (w c b) -> p b w c", w=2, b=2),
                )

            def copy_split(copy, a, b, split, i):
                halves = split[:, 2 * i * P : 2 * (i + 1) * P].bitcast(BF16).rearrange("p (w c e) -> p w c e", w=2, e=2)
                copy(out=grouped(a)[:, b, 1 - a, :, :], in_=halves[:, :, :, 1 - b])

            if shared:
                whole_0 = flip_whole(0)
                whole_1 = flip_whole(1)
                split_0 = flip_split(0, [0, 1])
                split_10 = flip_split(1, [0])
                split_11 = flip_split(1, [1])
                copy_whole(nc.scalar.copy, 0, whole_0)
                nc.scalar.copy(
                    out=grouped(0)[:, :, 1, :, :].rearrange("p b w c -> p b (w c)"),
                    in_=split_0[:].bitcast(BF16)[:, 1 : 8 * P - 1].rearrange("p (b r) -> p b r", b=2)[:, :, 0 : 4 * P - 1 : 2],
                )
                copy_split(nc.scalar.copy, 1, 1, split_11, 0)
                copy_whole(nc.vector.tensor_copy, 1, whole_1)
                copy_split(nc.vector.tensor_copy, 1, 0, split_10, 0)
            else:
                whole_0 = flip_whole(0)
                split_0 = flip_split(0, [0, 1])
                whole_1 = flip_whole(1)
                split_1 = flip_split(1, [0, 1])
                copy_whole(nc.scalar.copy, 0, whole_0)
                copy_split(nc.scalar.copy, 0, 0, split_0, 0)
                copy_split(nc.scalar.copy, 0, 1, split_0, 1)
                copy_split(nc.scalar.copy, 1, 0, split_1, 0)
                copy_split(nc.scalar.copy, 1, 1, split_1, 1)
                copy_whole(nc.vector.tensor_copy, 1, whole_1)
            for a in range(2):
                nc.vector.quantize_mx(
                    out=w_codes[:, 2 * a * COLS : 2 * (a + 1) * COLS].bitcast(FP8X4),
                    scales=w_scales[:, 2 * a * COLS : 2 * (a + 1) * COLS],
                    in_=grouped_tiles[a][:],
                )
            return w_codes, w_scales

        def multiply_and_store(first, operands):
            count = len(operands)
            sums = sum_banks.tile([P, count * COLS], F32)
            for i in range(count):
                w_codes, w_scales = operands[i]
                for s in range(PLACES):
                    nc.tensor.matmul_mx(
                        out=sums[:, i * COLS : (i + 1) * COLS],
                        lhsT=x_codes[:, s * P : (s + 1) * P].bitcast(FP8X4),
                        lhsT_scale=x_scales[:, s * P : (s + 1) * P],
                        rhs=w_codes[:, s * COLS : (s + 1) * COLS].bitcast(FP8X4),
                        rhs_scale=w_scales[:, s * COLS : (s + 1) * COLS],
                        start=(s == 0),
                        stop=(s == PLACES - 1),
                    )
            o_cols = slice(first * COLS, (first + count) * COLS)
            biased = work.tile([BATCH, count * COLS], F32)
            nc.vector.tensor_tensor(
                out=biased[:].rearrange("n (j ol hw) -> n j ol hw", j=count, hw=PLACES),
                in0=sums[0:BATCH, :].rearrange("n (j hw ol) -> n j ol hw", j=count, hw=PLACES),
                in1=bias_rows[:, o_cols].rearrange("n (j ol hw) -> n j ol hw", j=count, hw=PLACES),
                op=ALU.add,
            )
            result = work.tile([BATCH, count * COLS], F32)
            nc.vector.scalar_tensor_tensor(
                out=result[:], in0=biased[:], scalar=NEG_SLOPE, in1=biased[:], op0=ALU.mult, op1=ALU.max
            )
            nc.sync.dma_start(out=out_rows[:, o_cols], in_=result[:])

        ready = [flip_and_quantise(j, True) for j in range(3)]
        multiply_and_store(0, ready[0:2])
        ready.append(flip_and_quantise(3, True))
        multiply_and_store(2, ready[2:3])
        multiply_and_store(3, ready[3:4])
